import numpy as np
import ml_dtypes

BF16 = ml_dtypes.bfloat16


def bf(x):
    return np.asarray(x, np.float32).astype(BF16)


def f32(x):
    return np.asarray(x, np.float32)


def f64(x):
    return np.asarray(x).astype(np.float64)


def striped(idx):
    return np.tile(idx.reshape(-1, 16).T, (8, 1))


S, F, C, M, O, T, H, K, N = 2048, 1024, 128, 128, 1024, 3, 1024, 6, 6144
EPS = 1e-5


def setup_inputs():
    return {
        'trees': bf(np.random.standard_normal((S, F))),
        'enc_w': bf(np.random.standard_normal((F, C)) / np.sqrt(F)),
        'enc_b': f32(0.1 * np.random.standard_normal((C, 1))),
        'w1': bf(2.0 * np.random.standard_normal((C, T * M)) / np.sqrt(T * C)),
        'b1': f32(0.5 + 0.1 * np.random.standard_normal((M, 1))),
        'w2': bf(np.random.standard_normal((M, T * O)) * np.sqrt(2.0 / M)),
        'offs': striped(np.concatenate([np.random.permutation(S)[:H] for _ in range(K)])),
    }


def reference(trees, enc_w, enc_b, w1, b1, w2, offs):
    idx = offs[:16].T.reshape(-1)
    x0 = f64(enc_w).T @ f64(trees).T + f64(enc_b)
    y = f64(b1) + sum(f64(w1)[:, t * M:(t + 1) * M].T @ x0[:, idx[t * S:(t + 1) * S]] for t in range(T))
    mu = y.mean()
    sd = np.sqrt(((y - mu) ** 2).sum() / (y.size - 1))
    h = np.maximum((y - mu) / (sd + EPS), 0.0)
    return np.concatenate([f64(w2)[:, t * O:(t + 1) * O].T @ h for t in range(T)], axis=0)

@@ -1,0 +1,158 @@
+import concourse.mybir as mybir
+from concourse.masks import make_identity
+
+BF16, F32, U16 = mybir.dt.bfloat16, mybir.dt.float32, mybir.dt.uint16
+ACT = mybir.ActivationFunctionType
+ALU = mybir.AluOpType
+
+P = 128
+NODES = 2048
+FEATURES = 1024
+FEATURE_BLOCKS = FEATURES // P
+TAPS = 3
+OUT_ROWS = 3072
+OUT_BLOCKS = OUT_ROWS // P
+PIECE = 512
+PIECES = NODES // PIECE
+NODE_BLOCKS = NODES // P
+BLOCKS_IN_PIECE = PIECE // P
+COUNT = P * NODES
+EPS = 1e-5
+
+FLOPS = 2 * P * NODES * (FEATURES + TAPS * P + OUT_ROWS)
+
+
+def tile_net_latency_b_kernel(tc, trees, enc_w, enc_b, w1, b1, w2, offs, out):
+    nc = tc.nc
+    with (
+        tc.tile_pool(name="held", bufs=1) as held,
+        tc.tile_pool(name="staging", bufs=12) as staging,
+        tc.psum_pool(name="banks", bufs=7) as banks,
+        tc.psum_pool(name="moments", bufs=1) as moments,
+    ):
+        enc_w_sb = held.tile([P, FEATURE_BLOCKS, P], BF16, name="enc_w_sb")
+        as_loaded = []
+        for i in range(NODE_BLOCKS):
+            block = held.tile([P, FEATURES], BF16, name=f"as_loaded{i}")
+            queue = nc.sync if i % 2 == 0 else nc.scalar
+            queue.dma_start(block[:], trees[i * P : (i + 1) * P, :])
+            as_loaded.append(block)
+            if i == BLOCKS_IN_PIECE - 1:
+                nc.sync.dma_start(enc_w_sb[:], enc_w.rearrange("(a p) c -> p a c", p=P))
+        offsets = held.tile([P, TAPS * NODES // 16], U16, name="offsets")
+        nc.sync.dma_start(offsets[:], offs)
+        w1_sb = held.tile([P, TAPS * P], BF16, name="w1_sb")
+        nc.sync.dma_start(w1_sb[:], w1)
+        w2_sb = held.tile([P, OUT_ROWS], BF16, name="w2_sb")
+        nc.sync.dma_start(w2_sb[:], w2)
+        enc_b_sb = held.tile([P, 1], F32, name="enc_b_sb")
+        nc.sync.dma_start(enc_b_sb[:], enc_b)
+        b1_sb = held.tile([P, 1], F32, name="b1_sb")
+        nc.sync.dma_start(b1_sb[:], b1)
+
+        identity = held.tile([P, P], BF16, name="identity")
+        make_identity(nc, identity[:])
+
+        mean_over_partitions = held.tile([P, P], F32, name="mean_over_partitions")
+        nc.vector.memset(mean_over_partitions[:], 1.0 / P)
+
+        one = held.tile([P, 1], F32, name="one")
+        nc.vector.memset(one[:], 1.0)
+        sqrt_of_one = held.tile([P, 1], F32, name="sqrt_of_one")
+        nc.scalar.activation(sqrt_of_one[:], one[:], ACT.Sqrt)
+
+        turned = [
+            held.tile([P, FEATURE_BLOCKS, PIECE], BF16, name=f"turned{j}") for j in range(PIECES)
+        ]
+        x0 = held.tile([P, NODES], BF16, name="x0")
+
+        def turn(i):
+            in_psum = banks.tile([P, FEATURE_BLOCKS, P], BF16, name="in_psum", tag="bank")
+            for a in range(FEATURE_BLOCKS):
+                nc.tensor.transpose(in_psum[:, a, :], as_loaded[i][:, a * P : (a + 1) * P], identity[:])
+            j, k = divmod(i, BLOCKS_IN_PIECE)
+            nc.vector.tensor_copy(turned[j][:, :, k * P : (k + 1) * P], in_psum[:])
+
+        def encode(j):
+            cols = slice(j * PIECE, (j + 1) * PIECE)
+            x0_sum = banks.tile([P, PIECE], F32, name="x0_sum", tag="bank")
+            for a in range(FEATURE_BLOCKS):
+                nc.tensor.matmul(
+                    x0_sum[:],
+                    enc_w_sb[:, a, :],
+                    turned[j][:, a, :],
+                    start=(a == 0),
+                    stop=(a == FEATURE_BLOCKS - 1),
+                )
+            nc.scalar.activation(x0[:, cols], x0_sum[:], ACT.Identity, bias=enc_b_sb[:])
+
+        for j in range(PIECES + 1):
+            if j < PIECES:
+                for i in range(j * BLOCKS_IN_PIECE, (j + 1) * BLOCKS_IN_PIECE):
+                    turn(i)
+            if j > 0:
+                encode(j - 1)
+
+        y_less_b1 = []
+        piece_stats = held.tile([P, PIECES * 6], F32, name="piece_stats")
+        for j in range(PIECES):
+            y_sum = banks.tile([P, PIECE], F32, name=f"y_sum{j}", tag="bank")
+            for t in range(TAPS):
+                first = (t * NODES + j * PIECE) // 16
+                nc.tensor.matmul(
+                    y_sum[:],
+                    w1_sb[:, t * P : (t + 1) * P],
+                    x0[:].indirect(offsets[:, first : first + PIECE // 16]),
+                    start=(t == 0),
+                    stop=(t == TAPS - 1),
+                )
+            nc.vector.bn_stats(piece_stats[:, j * 6 : (j + 1) * 6], y_sum[:])
+            y_less_b1.append(y_sum)
+
+        row_mean_var = held.tile([P, 2], F32, name="row_mean_var")
+        nc.vector.bn_aggr(row_mean_var[:], piece_stats[:])
+        row_mean = held.tile([P, 1], F32, name="row_mean")
+        nc.vector.tensor_add(row_mean[:], row_mean_var[:, 0:1], b1_sb[:])
+        mu_and_var = moments.tile([P, 2], F32, name="mu_and_var")
+        nc.tensor.matmul(mu_and_var[:, 0:1], mean_over_partitions[:], row_mean[:])
+        b1_less_mu = held.tile([P, 1], F32, name="b1_less_mu")
+        nc.vector.tensor_sub(b1_less_mu[:], b1_sb[:], mu_and_var[:, 0:1])
+
+        row_dev = held.tile([P, 1], F32, name="row_dev")
+        nc.vector.tensor_sub(row_dev[:], row_mean[:], mu_and_var[:, 0:1])
+        row_spread = held.tile([P, 1], F32, name="row_spread")
+        nc.vector.scalar_tensor_tensor(
+            row_spread[:], row_dev[:], row_dev[:], row_mean_var[:, 1:2], op0=ALU.mult, op1=ALU.add
+        )
+        nc.tensor.matmul(mu_and_var[:, 1:2], mean_over_partitions[:], row_spread[:])
+
+        relu_y = []
+        for j in range(PIECES):
+            piece = held.tile([P, PIECE], BF16, name=f"relu_y{j}")
+            if j % 2 == 0:
+                nc.vector.tensor_scalar(
+                    piece[:], y_less_b1[j][:], b1_less_mu[:], 0.0, op0=ALU.add, op1=ALU.max
+                )
+            else:
+                nc.scalar.activation(piece[:], y_less_b1[j][:], ACT.Relu, bias=b1_less_mu[:])
+            relu_y.append(piece)
+
+        sd = held.tile([P, 1], F32, name="sd")
+        nc.scalar.activation(sd[:], mu_and_var[:, 1:2], ACT.Sqrt, scale=COUNT / (COUNT - 1.0))
+        sd_plus_eps = held.tile([P, 1], F32, name="sd_plus_eps")
+        nc.vector.tensor_scalar_add(sd_plus_eps[:], sd[:], EPS)
+        inv_sd = held.tile([P, 1], F32, name="inv_sd")
+        nc.vector.reciprocal(inv_sd[:], sd_plus_eps[:])
+
+        for half in range(PIECES // 2):
+            for b in range(OUT_BLOCKS):
+                rows = slice(b * P, (b + 1) * P)
+                staged = staging.tile([P, 2 * PIECE], F32, name="staged")
+                for k in range(2):
+                    product = banks.tile([P, PIECE], F32, name="product", tag="bank")
+                    nc.tensor.matmul(product[:], w2_sb[:, rows], relu_y[2 * half + k][:])
+                    if k == 0:
+                        nc.vector.tensor_scalar_mul(staged[:, :PIECE], product[:], inv_sd[:])
+                    else:
+                        nc.scalar.activation(staged[:, PIECE:], product[:], ACT.Copy, scale=inv_sd[:])
+                nc.sync.dma_start(out[rows, half * 2 * PIECE : (half + 1) * 2 * PIECE], staged[:])

@@ -69,7 +69,7 @@ def tile_net_latency_b_kernel(tc, trees, enc_w, enc_b, w1, b1, w2, offs, out):
         def turn(i):
             in_psum = banks.tile([P, FEATURE_BLOCKS, P], BF16, name="in_psum", tag="bank")
             for a in range(FEATURE_BLOCKS):
-                nc.tensor.transpose(in_psum[:, a, :], as_loaded[i][:, a * P : (a + 1) * P], identity[:])
+                nc.tensor.matmul(in_psum[:, a, :], as_loaded[i][:, a * P : (a + 1) * P], identity[:])
             j, k = divmod(i, BLOCKS_IN_PIECE)
             nc.vector.tensor_copy(turned[j][:, :, k * P : (k + 1) * P], in_psum[:])
 

@@ -14,7 +14,6 @@ OUT_ROWS = 3072
 OUT_BLOCKS = OUT_ROWS // P
 PIECE = 512
 PIECES = NODES // PIECE
-NODE_BLOCKS = NODES // P
 BLOCKS_IN_PIECE = PIECE // P
 COUNT = P * NODES
 EPS = 1e-5
@@ -26,29 +25,31 @@ def tile_net_latency_b_kernel(tc, trees, enc_w, enc_b, w1, b1, w2, offs, out):
     nc = tc.nc
     with (
         tc.tile_pool(name="held", bufs=1) as held,
-        tc.tile_pool(name="staging", bufs=12) as staging,
+        tc.tile_pool(name="staging", bufs=6) as staging,
         tc.psum_pool(name="banks", bufs=7) as banks,
         tc.psum_pool(name="moments", bufs=1) as moments,
     ):
+        as_loaded = [
+            held.tile([P, BLOCKS_IN_PIECE, FEATURES], BF16, name=f"as_loaded{j}") for j in range(PIECES)
+        ]
         enc_w_sb = held.tile([P, FEATURE_BLOCKS, P], BF16, name="enc_w_sb")
-        as_loaded = []
-        for i in range(NODE_BLOCKS):
-            block = held.tile([P, FEATURES], BF16, name=f"as_loaded{i}")
-            queue = nc.sync if i % 2 == 0 else nc.scalar
-            queue.dma_start(block[:], trees[i * P : (i + 1) * P, :])
-            as_loaded.append(block)
-            if i == BLOCKS_IN_PIECE - 1:
-                nc.sync.dma_start(enc_w_sb[:], enc_w.rearrange("(a p) c -> p a c", p=P))
-        offsets = held.tile([P, TAPS * NODES // 16], U16, name="offsets")
-        nc.sync.dma_start(offsets[:], offs)
-        w1_sb = held.tile([P, TAPS * P], BF16, name="w1_sb")
-        nc.sync.dma_start(w1_sb[:], w1)
-        w2_sb = held.tile([P, OUT_ROWS], BF16, name="w2_sb")
-        nc.sync.dma_start(w2_sb[:], w2)
         enc_b_sb = held.tile([P, 1], F32, name="enc_b_sb")
-        nc.sync.dma_start(enc_b_sb[:], enc_b)
+        offsets = held.tile([P, TAPS * NODES // 16], U16, name="offsets")
+        w1_sb = held.tile([P, TAPS * P], BF16, name="w1_sb")
         b1_sb = held.tile([P, 1], F32, name="b1_sb")
+        w2_sb = held.tile([P, OUT_ROWS], BF16, name="w2_sb")
+        for j in range(PIECES):
+            nc.sync.dma_start(
+                as_loaded[j][:],
+                trees[j * PIECE : (j + 1) * PIECE, :].rearrange("(k p) f -> p k f", p=P),
+            )
+            if j == 0:
+                nc.sync.dma_start(enc_w_sb[:], enc_w.rearrange("(a p) c -> p a c", p=P))
+                nc.sync.dma_start(enc_b_sb[:], enc_b)
+        nc.sync.dma_start(offsets[:], offs)
+        nc.sync.dma_start(w1_sb[:], w1)
         nc.sync.dma_start(b1_sb[:], b1)
+        nc.sync.dma_start(w2_sb[:], w2)
 
         identity = held.tile([P, P], BF16, name="identity")
         make_identity(nc, identity[:])
@@ -61,37 +62,45 @@ def tile_net_latency_b_kernel(tc, trees, enc_w, enc_b, w1, b1, w2, offs, out):
         sqrt_of_one = held.tile([P, 1], F32, name="sqrt_of_one")
         nc.scalar.activation(sqrt_of_one[:], one[:], ACT.Sqrt)
 
-        turned = [
-            held.tile([P, FEATURE_BLOCKS, PIECE], BF16, name=f"turned{j}") for j in range(PIECES)
-        ]
         x0 = held.tile([P, NODES], BF16, name="x0")
+        turned_tiles = []
+        x0_sums = []
 
-        def turn(i):
-            in_psum = banks.tile([P, FEATURE_BLOCKS, P], BF16, name="in_psum", tag="bank")
-            for a in range(FEATURE_BLOCKS):
-                nc.tensor.matmul(in_psum[:, a, :], as_loaded[i][:, a * P : (a + 1) * P], identity[:])
-            j, k = divmod(i, BLOCKS_IN_PIECE)
-            nc.vector.tensor_copy(turned[j][:, :, k * P : (k + 1) * P], in_psum[:])
-
-        def encode(j):
-            cols = slice(j * PIECE, (j + 1) * PIECE)
-            x0_sum = banks.tile([P, PIECE], F32, name="x0_sum", tag="bank")
-            for a in range(FEATURE_BLOCKS):
-                nc.tensor.matmul(
-                    x0_sum[:],
-                    enc_w_sb[:, a, :],
-                    turned[j][:, a, :],
-                    start=(a == 0),
-                    stop=(a == FEATURE_BLOCKS - 1),
+        def turn(j, a):
+            in_psum = banks.tile([P, PIECE], BF16, name="in_psum", tag="bank")
+            for k in range(BLOCKS_IN_PIECE):
+                nc.tensor.transpose(
+                    in_psum[:, k * P : (k + 1) * P], as_loaded[j][:, k, a * P : (a + 1) * P], identity[:]
                 )
-            nc.scalar.activation(x0[:, cols], x0_sum[:], ACT.Identity, bias=enc_b_sb[:])
+            turned = held.tile([P, PIECE], BF16, name=f"turned{j}_{a}")
+            if a % 2 == 0:
+                nc.vector.tensor_copy(turned[:], in_psum[:])
+            else:
+                nc.scalar.copy(turned[:], in_psum[:])
+            turned_tiles.append(turned)
 
-        for j in range(PIECES + 1):
-            if j < PIECES:
-                for i in range(j * BLOCKS_IN_PIECE, (j + 1) * BLOCKS_IN_PIECE):
-                    turn(i)
-            if j > 0:
-                encode(j - 1)
+        def add_share(j, a):
+            if a == 0:
+                x0_sums.append(banks.tile([P, PIECE], F32, name="x0_sum", tag="bank"))
+            nc.tensor.matmul(
+                x0_sums[j][:],
+                enc_w_sb[:, a, :],
+                turned_tiles[j * FEATURE_BLOCKS + a][:],
+                start=(a == 0),
+                stop=(a == FEATURE_BLOCKS - 1),
+            )
+            if a == FEATURE_BLOCKS - 1:
+                nc.scalar.activation(
+                    x0[:, j * PIECE : (j + 1) * PIECE], x0_sums[j][:], ACT.Identity, bias=enc_b_sb[:]
+                )
+
+        LEAD = 4
+        STEPS = PIECES * FEATURE_BLOCKS
+        for step in range(STEPS + LEAD):
+            if step < STEPS:
+                turn(step // FEATURE_BLOCKS, step % FEATURE_BLOCKS)
+            if step >= LEAD:
+                add_share((step - LEAD) // FEATURE_BLOCKS, (step - LEAD) % FEATURE_BLOCKS)
 
         y_less_b1 = []
         piece_stats = held.tile([P, PIECES * 6], F32, name="piece_stats")
@@ -144,15 +153,15 @@ def tile_net_latency_b_kernel(tc, trees, enc_w, enc_b, w1, b1, w2, offs, out):
         inv_sd = held.tile([P, 1], F32, name="inv_sd")
         nc.vector.reciprocal(inv_sd[:], sd_plus_eps[:])
 
-        for half in range(PIECES // 2):
-            for b in range(OUT_BLOCKS):
-                rows = slice(b * P, (b + 1) * P)
-                staged = staging.tile([P, 2 * PIECE], F32, name="staged")
-                for k in range(2):
-                    product = banks.tile([P, PIECE], F32, name="product", tag="bank")
-                    nc.tensor.matmul(product[:], w2_sb[:, rows], relu_y[2 * half + k][:])
-                    if k == 0:
-                        nc.vector.tensor_scalar_mul(staged[:, :PIECE], product[:], inv_sd[:])
-                    else:
-                        nc.scalar.activation(staged[:, PIECE:], product[:], ACT.Copy, scale=inv_sd[:])
-                nc.sync.dma_start(out[rows, half * 2 * PIECE : (half + 1) * 2 * PIECE], staged[:])
+        for b in range(OUT_BLOCKS):
+            rows = slice(b * P, (b + 1) * P)
+            staged = staging.tile([P, NODES], F32, name="staged")
+            for j in range(PIECES):
+                cols = slice(j * PIECE, (j + 1) * PIECE)
+                product = banks.tile([P, PIECE], F32, name="product", tag="bank")
+                nc.tensor.matmul(product[:], w2_sb[:, rows], relu_y[j][:])
+                if j % 2 == 0:
+                    nc.vector.tensor_scalar_mul(staged[:, cols], product[:], inv_sd[:])
+                else:
+                    nc.scalar.activation(staged[:, cols], product[:], ACT.Copy, scale=inv_sd[:])
+            nc.sync.dma_start(out[rows, :], staged[:])

@@ -56,6 +56,8 @@ def tile_net_latency_b_kernel(tc, trees, enc_w, enc_b, w1, b1, w2, offs, out):
 
         mean_over_partitions = held.tile([P, P], F32, name="mean_over_partitions")
         nc.vector.memset(mean_over_partitions[:], 1.0 / P)
+        minus_mean_of_means = held.tile([P, P], F32, name="minus_mean_of_means")
+        nc.vector.memset(minus_mean_of_means[:], -1.0 / (P * 2 * PIECES))
 
         one = held.tile([P, 1], F32, name="one")
         nc.vector.memset(one[:], 1.0)
@@ -102,6 +104,11 @@ def tile_net_latency_b_kernel(tc, trees, enc_w, enc_b, w1, b1, w2, offs, out):
             if step >= LEAD:
                 add_share((step - LEAD) // FEATURE_BLOCKS, (step - LEAD) % FEATURE_BLOCKS)
 
+        small_sums = moments.tile([P, 4], F32, name="small_sums")
+        nc.tensor.matmul(small_sums[:, 3:4], mean_over_partitions[:], b1_sb[:])
+        b1_centred = held.tile([P, 1], F32, name="b1_centred")
+        nc.vector.tensor_sub(b1_centred[:], b1_sb[:], small_sums[:, 3:4])
+
         y_less_b1 = []
         piece_stats = held.tile([P, PIECES * 6], F32, name="piece_stats")
         for j in range(PIECES):
@@ -118,24 +125,31 @@ def tile_net_latency_b_kernel(tc, trees, enc_w, enc_b, w1, b1, w2, offs, out):
             nc.vector.bn_stats(piece_stats[:, j * 6 : (j + 1) * 6], y_sum[:])
             y_less_b1.append(y_sum)
 
+        for j in range(PIECES):
+            nc.tensor.matmul(
+                small_sums[:, 0:2],
+                minus_mean_of_means[:],
+                piece_stats[:, j * 6 + 1 : j * 6 + 5 : 3],
+                start=(j == 0),
+                stop=(j == PIECES - 1),
+            )
         row_mean_var = held.tile([P, 2], F32, name="row_mean_var")
         nc.vector.bn_aggr(row_mean_var[:], piece_stats[:])
-        row_mean = held.tile([P, 1], F32, name="row_mean")
-        nc.vector.tensor_add(row_mean[:], row_mean_var[:, 0:1], b1_sb[:])
-        mu_and_var = moments.tile([P, 2], F32, name="mu_and_var")
-        nc.tensor.matmul(mu_and_var[:, 0:1], mean_over_partitions[:], row_mean[:])
         b1_less_mu = held.tile([P, 1], F32, name="b1_less_mu")
-        nc.vector.tensor_sub(b1_less_mu[:], b1_sb[:], mu_and_var[:, 0:1])
+        nc.vector.scalar_tensor_tensor(
+            b1_less_mu[:], small_sums[:, 0:1], small_sums[:, 1:2], b1_centred[:], op0=ALU.add, op1=ALU.add
+        )
 
         row_dev = held.tile([P, 1], F32, name="row_dev")
-        nc.vector.tensor_sub(row_dev[:], row_mean[:], mu_and_var[:, 0:1])
+        nc.vector.tensor_add(row_dev[:], row_mean_var[:, 0:1], b1_less_mu[:])
         row_spread = held.tile([P, 1], F32, name="row_spread")
         nc.vector.scalar_tensor_tensor(
             row_spread[:], row_dev[:], row_dev[:], row_mean_var[:, 1:2], op0=ALU.mult, op1=ALU.add
         )
-        nc.tensor.matmul(mu_and_var[:, 1:2], mean_over_partitions[:], row_spread[:])
+        nc.tensor.matmul(small_sums[:, 2:3], mean_over_partitions[:], row_spread[:])
 
         relu_y = []
+        sd = held.tile([P, 1], F32, name="sd")
         for j in range(PIECES):
             piece = held.tile([P, PIECE], BF16, name=f"relu_y{j}")
             if j % 2 == 0:
@@ -145,14 +159,14 @@ def tile_net_latency_b_kernel(tc, trees, enc_w, enc_b, w1, b1, w2, offs, out):
             else:
                 nc.scalar.activation(piece[:], y_less_b1[j][:], ACT.Relu, bias=b1_less_mu[:])
             relu_y.append(piece)
-
-        sd = held.tile([P, 1], F32, name="sd")
-        nc.scalar.activation(sd[:], mu_and_var[:, 1:2], ACT.Sqrt, scale=COUNT / (COUNT - 1.0))
+            if j == 1:
+                nc.scalar.activation(sd[:], small_sums[:, 2:3], ACT.Sqrt, scale=COUNT / (COUNT - 1.0))
         sd_plus_eps = held.tile([P, 1], F32, name="sd_plus_eps")
         nc.vector.tensor_scalar_add(sd_plus_eps[:], sd[:], EPS)
         inv_sd = held.tile([P, 1], F32, name="inv_sd")
         nc.vector.reciprocal(inv_sd[:], sd_plus_eps[:])
 
+        RAMP_BLOCKS = 3
         for b in range(OUT_BLOCKS):
             rows = slice(b * P, (b + 1) * P)
             staged = staging.tile([P, NODES], F32, name="staged")
@@ -164,4 +178,7 @@ def tile_net_latency_b_kernel(tc, trees, enc_w, enc_b, w1, b1, w2, offs, out):
                     nc.vector.tensor_scalar_mul(staged[:, cols], product[:], inv_sd[:])
                 else:
                     nc.scalar.activation(staged[:, cols], product[:], ACT.Copy, scale=inv_sd[:])
-            nc.sync.dma_start(out[rows, :], staged[:])
+                if b < RAMP_BLOCKS:
+                    nc.sync.dma_start(out[rows, cols], staged[:, cols])
+            if b >= RAMP_BLOCKS:
+                nc.sync.dma_start(out[rows, :], staged[:])

@@ -25,7 +25,8 @@ def tile_net_latency_b_kernel(tc, trees, enc_w, enc_b, w1, b1, w2, offs, out):
     nc = tc.nc
     with (
         tc.tile_pool(name="held", bufs=1) as held,
-        tc.tile_pool(name="staging", bufs=6) as staging,
+        tc.tile_pool(name="one_block", bufs=4) as one_block,
+        tc.tile_pool(name="many_blocks", bufs=3) as many_blocks,
         tc.psum_pool(name="banks", bufs=7) as banks,
         tc.psum_pool(name="moments", bufs=1) as moments,
     ):
@@ -56,8 +57,6 @@ def tile_net_latency_b_kernel(tc, trees, enc_w, enc_b, w1, b1, w2, offs, out):
 
         mean_over_partitions = held.tile([P, P], F32, name="mean_over_partitions")
         nc.vector.memset(mean_over_partitions[:], 1.0 / P)
-        minus_mean_of_means = held.tile([P, P], F32, name="minus_mean_of_means")
-        nc.vector.memset(minus_mean_of_means[:], -1.0 / (P * 2 * PIECES))
 
         one = held.tile([P, 1], F32, name="one")
         nc.vector.memset(one[:], 1.0)
@@ -104,11 +103,6 @@ def tile_net_latency_b_kernel(tc, trees, enc_w, enc_b, w1, b1, w2, offs, out):
             if step >= LEAD:
                 add_share((step - LEAD) // FEATURE_BLOCKS, (step - LEAD) % FEATURE_BLOCKS)
 
-        small_sums = moments.tile([P, 4], F32, name="small_sums")
-        nc.tensor.matmul(small_sums[:, 3:4], mean_over_partitions[:], b1_sb[:])
-        b1_centred = held.tile([P, 1], F32, name="b1_centred")
-        nc.vector.tensor_sub(b1_centred[:], b1_sb[:], small_sums[:, 3:4])
-
         y_less_b1 = []
         piece_stats = held.tile([P, PIECES * 6], F32, name="piece_stats")
         for j in range(PIECES):
@@ -125,28 +119,22 @@ def tile_net_latency_b_kernel(tc, trees, enc_w, enc_b, w1, b1, w2, offs, out):
             nc.vector.bn_stats(piece_stats[:, j * 6 : (j + 1) * 6], y_sum[:])
             y_less_b1.append(y_sum)
 
-        for j in range(PIECES):
-            nc.tensor.matmul(
-                small_sums[:, 0:2],
-                minus_mean_of_means[:],
-                piece_stats[:, j * 6 + 1 : j * 6 + 5 : 3],
-                start=(j == 0),
-                stop=(j == PIECES - 1),
-            )
         row_mean_var = held.tile([P, 2], F32, name="row_mean_var")
         nc.vector.bn_aggr(row_mean_var[:], piece_stats[:])
+        row_mean = held.tile([P, 1], F32, name="row_mean")
+        nc.vector.tensor_add(row_mean[:], row_mean_var[:, 0:1], b1_sb[:])
+        mu_and_var = moments.tile([P, 2], F32, name="mu_and_var")
+        nc.tensor.matmul(mu_and_var[:, 0:1], mean_over_partitions[:], row_mean[:])
         b1_less_mu = held.tile([P, 1], F32, name="b1_less_mu")
-        nc.vector.scalar_tensor_tensor(
-            b1_less_mu[:], small_sums[:, 0:1], small_sums[:, 1:2], b1_centred[:], op0=ALU.add, op1=ALU.add
-        )
+        nc.vector.tensor_sub(b1_less_mu[:], b1_sb[:], mu_and_var[:, 0:1])
 
         row_dev = held.tile([P, 1], F32, name="row_dev")
-        nc.vector.tensor_add(row_dev[:], row_mean_var[:, 0:1], b1_less_mu[:])
+        nc.vector.tensor_sub(row_dev[:], row_mean[:], mu_and_var[:, 0:1])
         row_spread = held.tile([P, 1], F32, name="row_spread")
         nc.vector.scalar_tensor_tensor(
             row_spread[:], row_dev[:], row_dev[:], row_mean_var[:, 1:2], op0=ALU.mult, op1=ALU.add
         )
-        nc.tensor.matmul(small_sums[:, 2:3], mean_over_partitions[:], row_spread[:])
+        nc.tensor.matmul(mu_and_var[:, 1:2], mean_over_partitions[:], row_spread[:])
 
         relu_y = []
         sd = held.tile([P, 1], F32, name="sd")
@@ -160,25 +148,35 @@ def tile_net_latency_b_kernel(tc, trees, enc_w, enc_b, w1, b1, w2, offs, out):
                 nc.scalar.activation(piece[:], y_less_b1[j][:], ACT.Relu, bias=b1_less_mu[:])
             relu_y.append(piece)
             if j == 1:
-                nc.scalar.activation(sd[:], small_sums[:, 2:3], ACT.Sqrt, scale=COUNT / (COUNT - 1.0))
+                nc.scalar.activation(sd[:], mu_and_var[:, 1:2], ACT.Sqrt, scale=COUNT / (COUNT - 1.0))
         sd_plus_eps = held.tile([P, 1], F32, name="sd_plus_eps")
         nc.vector.tensor_scalar_add(sd_plus_eps[:], sd[:], EPS)
         inv_sd = held.tile([P, 1], F32, name="inv_sd")
         nc.vector.reciprocal(inv_sd[:], sd_plus_eps[:])
 
-        RAMP_BLOCKS = 3
-        for b in range(OUT_BLOCKS):
-            rows = slice(b * P, (b + 1) * P)
-            staged = staging.tile([P, NODES], F32, name="staged")
-            for j in range(PIECES):
-                cols = slice(j * PIECE, (j + 1) * PIECE)
-                product = banks.tile([P, PIECE], F32, name="product", tag="bank")
-                nc.tensor.matmul(product[:], w2_sb[:, rows], relu_y[j][:])
-                if j % 2 == 0:
-                    nc.vector.tensor_scalar_mul(staged[:, cols], product[:], inv_sd[:])
-                else:
-                    nc.scalar.activation(staged[:, cols], product[:], ACT.Copy, scale=inv_sd[:])
-                if b < RAMP_BLOCKS:
-                    nc.sync.dma_start(out[rows, cols], staged[:, cols])
-            if b >= RAMP_BLOCKS:
-                nc.sync.dma_start(out[rows, :], staged[:])
+        STORE_PLAN = ((1, 4), (1, 2), (1, 1), (1, 1), (2, 1), (2, 1), (4, 1), (4, 1), (4, 1), (4, 1))
+        assert sum(blocks for blocks, parts in STORE_PLAN) == OUT_BLOCKS
+        first_block = 0
+        for blocks, parts in STORE_PLAN:
+            if blocks == 1:
+                staged = one_block.tile([P, blocks, NODES], F32, name="staged", tag="one_block")
+            else:
+                staged = many_blocks.tile([P, blocks, NODES], F32, name="staged", tag="many_blocks")
+            group_rows = out[first_block * P : (first_block + blocks) * P, :].rearrange(
+                "(e p) n -> p e n", p=P
+            )
+            for part in range(parts):
+                part_pieces = range(part * PIECES // parts, (part + 1) * PIECES // parts)
+                for e in range(blocks):
+                    rows = slice((first_block + e) * P, (first_block + e + 1) * P)
+                    for j in part_pieces:
+                        cols = slice(j * PIECE, (j + 1) * PIECE)
+                        product = banks.tile([P, PIECE], F32, name="product", tag="bank")
+                        nc.tensor.matmul(product[:], w2_sb[:, rows], relu_y[j][:])
+                        if j % 2 == 0:
+                            nc.vector.tensor_scalar_mul(staged[:, e, cols], product[:], inv_sd[:])
+                        else:
+                            nc.scalar.activation(staged[:, e, cols], product[:], ACT.Copy, scale=inv_sd[:])
+                part_cols = slice(part_pieces.start * PIECE, part_pieces.stop * PIECE)
+                nc.sync.dma_start(group_rows[:, :, part_cols], staged[:, :, part_cols])
+            first_block += blocks

@@ -162,13 +162,12 @@ def tile_net_latency_b_kernel(tc, trees, enc_w, enc_b, w1, b1, w2, offs, out):
                 staged = one_block.tile([P, blocks, NODES], F32, name="staged", tag="one_block")
             else:
                 staged = many_blocks.tile([P, blocks, NODES], F32, name="staged", tag="many_blocks")
-            group_rows = out[first_block * P : (first_block + blocks) * P, :].rearrange(
-                "(e p) n -> p e n", p=P
-            )
+            first_row = first_block * P
+            group_rows = out[first_row : first_row + blocks * P, :].rearrange("(p e) n -> p e n", e=blocks)
             for part in range(parts):
                 part_pieces = range(part * PIECES // parts, (part + 1) * PIECES // parts)
                 for e in range(blocks):
-                    rows = slice((first_block + e) * P, (first_block + e + 1) * P)
+                    rows = slice(first_row + e, first_row + blocks * P, blocks)
                     for j in part_pieces:
                         cols = slice(j * PIECE, (j + 1) * PIECE)
                         product = banks.tile([P, PIECE], F32, name="product", tag="bank")

@@ -14,7 +14,9 @@ OUT_ROWS = 3072
 OUT_BLOCKS = OUT_ROWS // P
 PIECE = 512
 PIECES = NODES // PIECE
-BLOCKS_IN_PIECE = PIECE // P
+SLICE = 256
+SLICES = NODES // SLICE
+BLOCKS_IN_SLICE = SLICE // P
 COUNT = P * NODES
 EPS = 1e-5
 
@@ -31,7 +33,7 @@ def tile_net_latency_b_kernel(tc, trees, enc_w, enc_b, w1, b1, w2, offs, out):
         tc.psum_pool(name="moments", bufs=1) as moments,
     ):
         as_loaded = [
-            held.tile([P, BLOCKS_IN_PIECE, FEATURES], BF16, name=f"as_loaded{j}") for j in range(PIECES)
+            held.tile([P, BLOCKS_IN_SLICE, FEATURES], BF16, name=f"as_loaded{i}") for i in range(SLICES)
         ]
         enc_w_sb = held.tile([P, FEATURE_BLOCKS, P], BF16, name="enc_w_sb")
         enc_b_sb = held.tile([P, 1], F32, name="enc_b_sb")
@@ -39,12 +41,12 @@ def tile_net_latency_b_kernel(tc, trees, enc_w, enc_b, w1, b1, w2, offs, out):
         w1_sb = held.tile([P, TAPS * P], BF16, name="w1_sb")
         b1_sb = held.tile([P, 1], F32, name="b1_sb")
         w2_sb = held.tile([P, OUT_ROWS], BF16, name="w2_sb")
-        for j in range(PIECES):
+        for i in range(SLICES):
             nc.sync.dma_start(
-                as_loaded[j][:],
-                trees[j * PIECE : (j + 1) * PIECE, :].rearrange("(k p) f -> p k f", p=P),
+                as_loaded[i][:],
+                trees[i * SLICE : (i + 1) * SLICE, :].rearrange("(k p) f -> p k f", p=P),
             )
-            if j == 0:
+            if i == 0:
                 nc.sync.dma_start(enc_w_sb[:], enc_w.rearrange("(a p) c -> p a c", p=P))
                 nc.sync.dma_start(enc_b_sb[:], enc_b)
         nc.sync.dma_start(offsets[:], offs)
@@ -67,36 +69,36 @@ def tile_net_latency_b_kernel(tc, trees, enc_w, enc_b, w1, b1, w2, offs, out):
         turned_tiles = []
         x0_sums = []
 
-        def turn(j, a):
-            in_psum = banks.tile([P, PIECE], BF16, name="in_psum", tag="bank")
-            for k in range(BLOCKS_IN_PIECE):
+        def turn(i, a):
+            in_psum = banks.tile([P, SLICE], BF16, name="in_psum", tag="bank")
+            for k in range(BLOCKS_IN_SLICE):
                 nc.tensor.transpose(
-                    in_psum[:, k * P : (k + 1) * P], as_loaded[j][:, k, a * P : (a + 1) * P], identity[:]
+                    in_psum[:, k * P : (k + 1) * P], as_loaded[i][:, k, a * P : (a + 1) * P], identity[:]
                 )
-            turned = held.tile([P, PIECE], BF16, name=f"turned{j}_{a}")
+            turned = held.tile([P, SLICE], BF16, name=f"turned{i}_{a}")
             if a % 2 == 0:
                 nc.vector.tensor_copy(turned[:], in_psum[:])
             else:
                 nc.scalar.copy(turned[:], in_psum[:])
             turned_tiles.append(turned)
 
-        def add_share(j, a):
+        def add_share(i, a):
             if a == 0:
-                x0_sums.append(banks.tile([P, PIECE], F32, name="x0_sum", tag="bank"))
+                x0_sums.append(banks.tile([P, SLICE], F32, name="x0_sum", tag="bank"))
             nc.tensor.matmul(
-                x0_sums[j][:],
+                x0_sums[i][:],
                 enc_w_sb[:, a, :],
-                turned_tiles[j * FEATURE_BLOCKS + a][:],
+                turned_tiles[i * FEATURE_BLOCKS + a][:],
                 start=(a == 0),
                 stop=(a == FEATURE_BLOCKS - 1),
             )
             if a == FEATURE_BLOCKS - 1:
                 nc.scalar.activation(
-                    x0[:, j * PIECE : (j + 1) * PIECE], x0_sums[j][:], ACT.Identity, bias=enc_b_sb[:]
+                    x0[:, i * SLICE : (i + 1) * SLICE], x0_sums[i][:], ACT.Identity, bias=enc_b_sb[:]
                 )
 
-        LEAD = 4
-        STEPS = PIECES * FEATURE_BLOCKS
+        LEAD = 6
+        STEPS = SLICES * FEATURE_BLOCKS
         for step in range(STEPS + LEAD):
             if step < STEPS:
                 turn(step // FEATURE_BLOCKS, step % FEATURE_BLOCKS)

@@ -93,8 +93,8 @@ def tile_net_latency_b_kernel(tc, trees, enc_w, enc_b, w1, b1, w2, offs, out):
                 stop=(a == FEATURE_BLOCKS - 1),
             )
             if a == FEATURE_BLOCKS - 1:
-                nc.scalar.activation(
-                    x0[:, i * SLICE : (i + 1) * SLICE], x0_sums[i][:], ACT.Identity, bias=enc_b_sb[:]
+                nc.vector.tensor_scalar_add(
+                    x0[:, i * SLICE : (i + 1) * SLICE], x0_sums[i][:], enc_b_sb[:]
                 )
 
         LEAD = 6

@@ -18,6 +18,7 @@ SLICE = 256
 SLICES = NODES // SLICE
 BLOCKS_IN_SLICE = SLICE // P
 COUNT = P * NODES
+DMA_ALIGN = 256
 EPS = 1e-5
 
 FLOPS = 2 * P * NODES * (FEATURES + TAPS * P + OUT_ROWS)
@@ -33,9 +34,10 @@ def tile_net_latency_b_kernel(tc, trees, enc_w, enc_b, w1, b1, w2, offs, out):
         tc.psum_pool(name="moments", bufs=1) as moments,
     ):
         as_loaded = [
-            held.tile([P, BLOCKS_IN_SLICE, FEATURES], BF16, name=f"as_loaded{i}") for i in range(SLICES)
+            held.tile([P, BLOCKS_IN_SLICE, FEATURES], BF16, name=f"as_loaded{i}", align_bytes=DMA_ALIGN)
+            for i in range(SLICES)
         ]
-        enc_w_sb = held.tile([P, FEATURE_BLOCKS, P], BF16, name="enc_w_sb")
+        enc_w_sb = held.tile([P, FEATURE_BLOCKS, P], BF16, name="enc_w_sb", align_bytes=DMA_ALIGN)
         enc_b_sb = held.tile([P, 1], F32, name="enc_b_sb")
         offsets = held.tile([P, TAPS * NODES // 16], U16, name="offsets")
         w1_sb = held.tile([P, TAPS * P], BF16, name="w1_sb")
@@ -161,9 +163,13 @@ def tile_net_latency_b_kernel(tc, trees, enc_w, enc_b, w1, b1, w2, offs, out):
         first_block = 0
         for blocks, parts in STORE_PLAN:
             if blocks == 1:
-                staged = one_block.tile([P, blocks, NODES], F32, name="staged", tag="one_block")
+                staged = one_block.tile(
+                    [P, blocks, NODES], F32, name="staged", tag="one_block", align_bytes=DMA_ALIGN
+                )
             else:
-                staged = many_blocks.tile([P, blocks, NODES], F32, name="staged", tag="many_blocks")
+                staged = many_blocks.tile(
+                    [P, blocks, NODES], F32, name="staged", tag="many_blocks", align_bytes=DMA_ALIGN
+                )
             first_row = first_block * P
             group_rows = out[first_row : first_row + blocks * P, :].rearrange("(p e) n -> p e n", e=blocks)
             for part in range(parts):

@@ -46,7 +46,7 @@ def tile_net_latency_b_kernel(tc, trees, enc_w, enc_b, w1, b1, w2, offs, out):
         for i in range(SLICES):
             nc.sync.dma_start(
                 as_loaded[i][:],
-                trees[i * SLICE : (i + 1) * SLICE, :].rearrange("(k p) f -> p k f", p=P),
+                trees[i * SLICE : (i + 1) * SLICE, :].rearrange("(p k) f -> p k f", p=P),
             )
             if i == 0:
                 nc.sync.dma_start(enc_w_sb[:], enc_w.rearrange("(a p) c -> p a c", p=P))
@@ -96,7 +96,9 @@ def tile_net_latency_b_kernel(tc, trees, enc_w, enc_b, w1, b1, w2, offs, out):
             )
             if a == FEATURE_BLOCKS - 1:
                 nc.vector.tensor_scalar_add(
-                    x0[:, i * SLICE : (i + 1) * SLICE], x0_sums[i][:], enc_b_sb[:]
+                    x0[:, i * SLICE : (i + 1) * SLICE].rearrange("c (q k) -> c q k", k=BLOCKS_IN_SLICE),
+                    x0_sums[i][:].rearrange("c (k q) -> c q k", k=BLOCKS_IN_SLICE),
+                    enc_b_sb[:],
                 )
 
         LEAD = 6

@@ -109,24 +109,27 @@ def tile_net_latency_b_kernel(tc, trees, enc_w, enc_b, w1, b1, w2, offs, out):
             if step >= LEAD:
                 add_share((step - LEAD) // FEATURE_BLOCKS, (step - LEAD) % FEATURE_BLOCKS)
 
+        PART_WIDTHS = (PIECE,) * (PIECES - 1) + (PIECE // 2,) * 2
+        PARTS = len(PART_WIDTHS)
+        part_first = [sum(PART_WIDTHS[:i]) for i in range(PARTS)]
         y_less_b1 = []
-        piece_stats = held.tile([P, PIECES * 6], F32, name="piece_stats")
-        for j in range(PIECES):
-            y_sum = banks.tile([P, PIECE], F32, name=f"y_sum{j}", tag="bank")
+        part_stats = held.tile([P, PARTS * 6], F32, name="part_stats")
+        for i in range(PARTS):
+            y_sum = banks.tile([P, PART_WIDTHS[i]], F32, name=f"y_sum{i}", tag="bank")
             for t in range(TAPS):
-                first = (t * NODES + j * PIECE) // 16
+                first = (t * NODES + part_first[i]) // 16
                 nc.tensor.matmul(
                     y_sum[:],
                     w1_sb[:, t * P : (t + 1) * P],
-                    x0[:].indirect(offsets[:, first : first + PIECE // 16]),
+                    x0[:].indirect(offsets[:, first : first + PART_WIDTHS[i] // 16]),
                     start=(t == 0),
                     stop=(t == TAPS - 1),
                 )
-            nc.vector.bn_stats(piece_stats[:, j * 6 : (j + 1) * 6], y_sum[:])
+            nc.vector.bn_stats(part_stats[:, i * 6 : (i + 1) * 6], y_sum[:])
             y_less_b1.append(y_sum)
 
         row_mean_var = held.tile([P, 2], F32, name="row_mean_var")
-        nc.vector.bn_aggr(row_mean_var[:], piece_stats[:])
+        nc.vector.bn_aggr(row_mean_var[:], part_stats[:])
         row_mean = held.tile([P, 1], F32, name="row_mean")
         nc.vector.tensor_add(row_mean[:], row_mean_var[:, 0:1], b1_sb[:])
         mu_and_var = moments.tile([P, 2], F32, name="mu_and_var")
@@ -142,19 +145,21 @@ def tile_net_latency_b_kernel(tc, trees, enc_w, enc_b, w1, b1, w2, offs, out):
         )
         nc.tensor.matmul(mu_and_var[:, 1:2], mean_over_partitions[:], row_spread[:])
 
-        relu_y = []
-        sd = held.tile([P, 1], F32, name="sd")
-        for j in range(PIECES):
-            piece = held.tile([P, PIECE], BF16, name=f"relu_y{j}")
-            if j % 2 == 0:
-                nc.vector.tensor_scalar(
-                    piece[:], y_less_b1[j][:], b1_less_mu[:], 0.0, op0=ALU.add, op1=ALU.max
-                )
+        relu_y = [held.tile([P, PIECE], BF16, name=f"relu_y{j}") for j in range(PIECES)]
+
+        def rectify(i):
+            j, first = divmod(part_first[i], PIECE)
+            rectified = relu_y[j][:, first : first + PART_WIDTHS[i]]
+            if i % 2 == 0:
+                nc.scalar.activation(rectified, y_less_b1[i][:], ACT.Relu, bias=b1_less_mu[:])
             else:
-                nc.scalar.activation(piece[:], y_less_b1[j][:], ACT.Relu, bias=b1_less_mu[:])
-            relu_y.append(piece)
-            if j == 1:
-                nc.scalar.activation(sd[:], mu_and_var[:, 1:2], ACT.Sqrt, scale=COUNT / (COUNT - 1.0))
+                nc.vector.tensor_scalar(rectified, y_less_b1[i][:], b1_less_mu[:], 0.0, op0=ALU.add, op1=ALU.max)
+
+        sd = held.tile([P, 1], F32, name="sd")
+        rectify(0)
+        rectify(1)
+        nc.scalar.activation(sd[:], mu_and_var[:, 1:2], ACT.Sqrt, scale=COUNT / (COUNT - 1.0))
+        rectify(2)
         sd_plus_eps = held.tile([P, 1], F32, name="sd_plus_eps")
         nc.vector.tensor_scalar_add(sd_plus_eps[:], sd[:], EPS)
         inv_sd = held.tile([P, 1], F32, name="inv_sd")
@@ -186,6 +191,8 @@ def tile_net_latency_b_kernel(tc, trees, enc_w, enc_b, w1, b1, w2, offs, out):
                             nc.vector.tensor_scalar_mul(staged[:, e, cols], product[:], inv_sd[:])
                         else:
                             nc.scalar.activation(staged[:, e, cols], product[:], ACT.Copy, scale=inv_sd[:])
+                        if first_block == 0 and j < 2:
+                            rectify(PIECES - 1 + j)
                 part_cols = slice(part_pieces.start * PIECE, part_pieces.stop * PIECE)
                 nc.sync.dma_start(group_rows[:, :, part_cols], staged[:, :, part_cols])
             first_block += blocks

@@ -132,18 +132,16 @@ def tile_net_latency_b_kernel(tc, trees, enc_w, enc_b, w1, b1, w2, offs, out):
         nc.vector.bn_aggr(row_mean_var[:], part_stats[:])
         row_mean = held.tile([P, 1], F32, name="row_mean")
         nc.vector.tensor_add(row_mean[:], row_mean_var[:, 0:1], b1_sb[:])
-        mu_and_var = moments.tile([P, 2], F32, name="mu_and_var")
+        mu_and_var = moments.tile([P, 1], F32, name="mu_and_var")
         nc.tensor.matmul(mu_and_var[:, 0:1], mean_over_partitions[:], row_mean[:])
         b1_less_mu = held.tile([P, 1], F32, name="b1_less_mu")
         nc.vector.tensor_sub(b1_less_mu[:], b1_sb[:], mu_and_var[:, 0:1])
 
-        row_dev = held.tile([P, 1], F32, name="row_dev")
-        nc.vector.tensor_sub(row_dev[:], row_mean[:], mu_and_var[:, 0:1])
-        row_spread = held.tile([P, 1], F32, name="row_spread")
-        nc.vector.scalar_tensor_tensor(
-            row_spread[:], row_dev[:], row_dev[:], row_mean_var[:, 1:2], op0=ALU.mult, op1=ALU.add
-        )
-        nc.tensor.matmul(mu_and_var[:, 1:2], mean_over_partitions[:], row_spread[:])
+        var_sum = banks.tile([P, 1], F32, name="var_sum", tag="bank")
+        nc.tensor.matmul(var_sum[:], mean_over_partitions[:], row_mean_var[:, 1:2], start=True, stop=False)
+        row_dev_squared = held.tile([P, 1], F32, name="row_dev_squared")
+        nc.scalar.activation(row_dev_squared[:], mu_and_var[:, 0:1], ACT.Square, bias=row_mean[:], scale=-1.0)
+        nc.tensor.matmul(var_sum[:], mean_over_partitions[:], row_dev_squared[:], start=False, stop=True)
 
         relu_y = [held.tile([P, PIECE], BF16, name=f"relu_y{j}") for j in range(PIECES)]
 
@@ -158,7 +156,7 @@ def tile_net_latency_b_kernel(tc, trees, enc_w, enc_b, w1, b1, w2, offs, out):
         sd = held.tile([P, 1], F32, name="sd")
         rectify(0)
         rectify(1)
-        nc.scalar.activation(sd[:], mu_and_var[:, 1:2], ACT.Sqrt, scale=COUNT / (COUNT - 1.0))
+        nc.scalar.activation(sd[:], var_sum[:], ACT.Sqrt, scale=COUNT / (COUNT - 1.0))
         rectify(2)
         sd_plus_eps = held.tile([P, 1], F32, name="sd_plus_eps")
         nc.vector.tensor_scalar_add(sd_plus_eps[:], sd[:], EPS)

import concourse.mybir as mybir
from concourse.masks import make_identity

BF16, F32, U16 = mybir.dt.bfloat16, mybir.dt.float32, mybir.dt.uint16
ACT = mybir.ActivationFunctionType
ALU = mybir.AluOpType

P = 128
NODES = 2048
FEATURES = 1024
FEATURE_BLOCKS = FEATURES // P
TAPS = 3
OUT_ROWS = 3072
OUT_BLOCKS = OUT_ROWS // P
PIECE = 512
PIECES = NODES // PIECE
SLICE = 256
SLICES = NODES // SLICE
BLOCKS_IN_SLICE = SLICE // P
COUNT = P * NODES
DMA_ALIGN = 256
EPS = 1e-5

FLOPS = 2 * P * NODES * (FEATURES + TAPS * P + OUT_ROWS)


def tile_net_latency_b_kernel(tc, trees, enc_w, enc_b, w1, b1, w2, offs, out):
    nc = tc.nc
    with (
        tc.tile_pool(name="held", bufs=1) as held,
        tc.tile_pool(name="one_block", bufs=4) as one_block,
        tc.tile_pool(name="many_blocks", bufs=3) as many_blocks,
        tc.psum_pool(name="banks", bufs=7) as banks,
        tc.psum_pool(name="moments", bufs=1) as moments,
    ):
        as_loaded = [
            held.tile([P, BLOCKS_IN_SLICE, FEATURES], BF16, name=f"as_loaded{i}", align_bytes=DMA_ALIGN)
            for i in range(SLICES)
        ]
        enc_w_sb = held.tile([P, FEATURE_BLOCKS, P], BF16, name="enc_w_sb", align_bytes=DMA_ALIGN)
        enc_b_sb = held.tile([P, 1], F32, name="enc_b_sb")
        offsets = held.tile([P, TAPS * NODES // 16], U16, name="offsets")
        w1_sb = held.tile([P, TAPS * P], BF16, name="w1_sb")
        b1_sb = held.tile([P, 1], F32, name="b1_sb")
        w2_sb = held.tile([P, OUT_ROWS], BF16, name="w2_sb")
        for i in range(SLICES):
            nc.sync.dma_start(
                as_loaded[i][:],
                trees[i * SLICE : (i + 1) * SLICE, :].rearrange("(p k) f -> p k f", p=P),
            )
            if i == 0:
                nc.sync.dma_start(enc_w_sb[:], enc_w.rearrange("(a p) c -> p a c", p=P))
                nc.sync.dma_start(enc_b_sb[:], enc_b)
        nc.sync.dma_start(offsets[:], offs)
        nc.sync.dma_start(w1_sb[:], w1)
        nc.sync.dma_start(b1_sb[:], b1)
        nc.sync.dma_start(w2_sb[:], w2)

        identity = held.tile([P, P], BF16, name="identity")
        make_identity(nc, identity[:])

        mean_over_partitions = held.tile([P, P], F32, name="mean_over_partitions")
        nc.vector.memset(mean_over_partitions[:], 1.0 / P)

        one = held.tile([P, 1], F32, name="one")
        nc.vector.memset(one[:], 1.0)
        sqrt_of_one = held.tile([P, 1], F32, name="sqrt_of_one")
        nc.scalar.activation(sqrt_of_one[:], one[:], ACT.Sqrt)

        x0 = held.tile([P, NODES], BF16, name="x0")
        turned_tiles = []
        x0_sums = []

        def turn(i, a):
            in_psum = banks.tile([P, SLICE], BF16, name="in_psum", tag="bank")
            for k in range(BLOCKS_IN_SLICE):
                nc.tensor.transpose(
                    in_psum[:, k * P : (k + 1) * P], as_loaded[i][:, k, a * P : (a + 1) * P], identity[:]
                )
            turned = held.tile([P, SLICE], BF16, name=f"turned{i}_{a}")
            if a % 2 == 0:
                nc.vector.tensor_copy(turned[:], in_psum[:])
            else:
                nc.scalar.copy(turned[:], in_psum[:])
            turned_tiles.append(turned)

        def add_share(i, a):
            if a == 0:
                x0_sums.append(banks.tile([P, SLICE], F32, name="x0_sum", tag="bank"))
            nc.tensor.matmul(
                x0_sums[i][:],
                enc_w_sb[:, a, :],
                turned_tiles[i * FEATURE_BLOCKS + a][:],
                start=(a == 0),
                stop=(a == FEATURE_BLOCKS - 1),
            )
            if a == FEATURE_BLOCKS - 1:
                nc.vector.tensor_scalar_add(
                    x0[:, i * SLICE : (i + 1) * SLICE].rearrange("c (q k) -> c q k", k=BLOCKS_IN_SLICE),
                    x0_sums[i][:].rearrange("c (k q) -> c q k", k=BLOCKS_IN_SLICE),
                    enc_b_sb[:],
                )

        LEAD = 6
        STEPS = SLICES * FEATURE_BLOCKS
        for step in range(STEPS + LEAD):
            if step < STEPS:
                turn(step // FEATURE_BLOCKS, step % FEATURE_BLOCKS)
            if step >= LEAD:
                add_share((step - LEAD) // FEATURE_BLOCKS, (step - LEAD) % FEATURE_BLOCKS)

        PART_WIDTHS = (PIECE,) * (PIECES - 1) + (PIECE // 2,) * 2
        PARTS = len(PART_WIDTHS)
        part_first = [sum(PART_WIDTHS[:i]) for i in range(PARTS)]
        y_less_b1 = []
        part_stats = held.tile([P, PARTS * 6], F32, name="part_stats")
        for i in range(PARTS):
            y_sum = banks.tile([P, PART_WIDTHS[i]], F32, name=f"y_sum{i}", tag="bank")
            for t in range(TAPS):
                first = (t * NODES + part_first[i]) // 16
                nc.tensor.matmul(
                    y_sum[:],
                    w1_sb[:, t * P : (t + 1) * P],
                    x0[:].indirect(offsets[:, first : first + PART_WIDTHS[i] // 16]),
                    start=(t == 0),
                    stop=(t == TAPS - 1),
                )
            nc.vector.bn_stats(part_stats[:, i * 6 : (i + 1) * 6], y_sum[:])
            y_less_b1.append(y_sum)

        row_mean_var = held.tile([P, 2], F32, name="row_mean_var")
        nc.vector.bn_aggr(row_mean_var[:], part_stats[:])
        row_mean = held.tile([P, 1], F32, name="row_mean")
        nc.vector.tensor_add(row_mean[:], row_mean_var[:, 0:1], b1_sb[:])
        mu_and_var = moments.tile([P, 1], F32, name="mu_and_var")
        nc.tensor.matmul(mu_and_var[:, 0:1], mean_over_partitions[:], row_mean[:])
        b1_less_mu = held.tile([P, 1], F32, name="b1_less_mu")
        nc.vector.tensor_sub(b1_less_mu[:], b1_sb[:], mu_and_var[:, 0:1])

        var_sum = banks.tile([P, 1], F32, name="var_sum", tag="bank")
        nc.tensor.matmul(var_sum[:], mean_over_partitions[:], row_mean_var[:, 1:2], start=True, stop=False)
        row_dev_squared = held.tile([P, 1], F32, name="row_dev_squared")
        nc.scalar.activation(row_dev_squared[:], mu_and_var[:, 0:1], ACT.Square, bias=row_mean[:], scale=-1.0)
        nc.tensor.matmul(var_sum[:], mean_over_partitions[:], row_dev_squared[:], start=False, stop=True)

        relu_y = [held.tile([P, PIECE], BF16, name=f"relu_y{j}") for j in range(PIECES)]

        def rectify(i):
            j, first = divmod(part_first[i], PIECE)
            rectified = relu_y[j][:, first : first + PART_WIDTHS[i]]
            if i % 2 == 0:
                nc.scalar.activation(rectified, y_less_b1[i][:], ACT.Relu, bias=b1_less_mu[:])
            else:
                nc.vector.tensor_scalar(rectified, y_less_b1[i][:], b1_less_mu[:], 0.0, op0=ALU.add, op1=ALU.max)

        sd = held.tile([P, 1], F32, name="sd")
        rectify(0)
        rectify(1)
        nc.scalar.activation(sd[:], var_sum[:], ACT.Sqrt, scale=COUNT / (COUNT - 1.0))
        rectify(2)
        sd_plus_eps = held.tile([P, 1], F32, name="sd_plus_eps")
        nc.vector.tensor_scalar_add(sd_plus_eps[:], sd[:], EPS)
        inv_sd = held.tile([P, 1], F32, name="inv_sd")
        nc.vector.reciprocal(inv_sd[:], sd_plus_eps[:])

        STORE_PLAN = ((1, 4), (1, 2), (1, 1), (1, 1), (2, 1), (2, 1), (4, 1), (4, 1), (4, 1), (4, 1))
        assert sum(blocks for blocks, parts in STORE_PLAN) == OUT_BLOCKS
        first_block = 0
        for blocks, parts in STORE_PLAN:
            if blocks == 1:
                staged = one_block.tile(
                    [P, blocks, NODES], F32, name="staged", tag="one_block", align_bytes=DMA_ALIGN
                )
            else:
                staged = many_blocks.tile(
                    [P, blocks, NODES], F32, name="staged", tag="many_blocks", align_bytes=DMA_ALIGN
                )
            first_row = first_block * P
            group_rows = out[first_row : first_row + blocks * P, :].rearrange("(p e) n -> p e n", e=blocks)
            for part in range(parts):
                part_pieces = range(part * PIECES // parts, (part + 1) * PIECES // parts)
                for e in range(blocks):
                    rows = slice(first_row + e, first_row + blocks * P, blocks)
                    for j in part_pieces:
                        cols = slice(j * PIECE, (j + 1) * PIECE)
                        product = banks.tile([P, PIECE], F32, name="product", tag="bank")
                        nc.tensor.matmul(product[:], w2_sb[:, rows], relu_y[j][:])
                        if j % 2 == 0:
                            nc.vector.tensor_scalar_mul(staged[:, e, cols], product[:], inv_sd[:])
                        else:
                            nc.scalar.activation(staged[:, e, cols], product[:], ACT.Copy, scale=inv_sd[:])
                        if first_block == 0 and j < 2:
                            rectify(PIECES - 1 + j)
                part_cols = slice(part_pieces.start * PIECE, part_pieces.stop * PIECE)
                nc.sync.dma_start(group_rows[:, :, part_cols], staged[:, :, part_cols])
            first_block += blocks
